import numpy as np
import ml_dtypes


def mxq(x, axis, fmt="e4m3"):
    dtype, down = {"e4m3": (ml_dtypes.float8_e4m3fn, 7), "e5m2": (ml_dtypes.float8_e5m2, 14)}[fmt]
    v = np.moveaxis(np.asarray(x, np.float32).astype(ml_dtypes.bfloat16).astype(np.float64), axis, -1)
    blocks = v.reshape(v.shape[:-1] + (-1, 32))
    amax = np.abs(blocks).max(-1, keepdims=True)
    byte = np.maximum(np.where(amax > 0, np.frexp(amax)[1] - 1 + 127, 0) - down, 1)
    scale = np.exp2(byte - 127.0)
    codes = (blocks / scale).astype(np.float32).astype(dtype).astype(np.float64)
    return np.moveaxis((codes * scale).reshape(v.shape), -1, axis)


WIDE = False


def mx_kscale(k):
    if not WIDE:
        return np.ones(k)
    levels = np.array([10, -10, 5, -5, 0])
    if k % 512:
        return np.exp2(np.random.permutation(np.resize(levels, k // 32))).repeat(32)
    a = np.empty((k // 512, 16))
    for p in range(k // 512):
        a[p, :8] = np.random.permutation(np.resize(levels, 8))
        for g in range(8):
            far = levels[np.abs(levels - a[p, g]) >= 10]
            a[p, g + 8] = far[np.random.randint(len(far))]
    return np.exp2(a.ravel()).repeat(32)


BF16 = ml_dtypes.bfloat16


def bf(x):
    return np.asarray(x, np.float32).astype(BF16)


def f64(x):
    return np.asarray(x).astype(np.float64)


B, C, HH, WW, NH, HD, F = 4, 512, 16, 16, 8, 64, 2048
EPS = 1e-5


def layer_norm(v, w, b):
    mu = v.mean(-1, keepdims=True)
    var = ((v - mu) ** 2).mean(-1, keepdims=True)
    return (v - mu) * (1.0 / np.sqrt(var + EPS)) * w + b


def setup_inputs():
    s = mx_kscale(F)
    return {"h": bf(np.maximum(np.random.standard_normal((B, HH, WW, F)), 0.0) * 0.125 * s),
            "ffn2_w": bf(np.random.standard_normal((C, F)) * 0.5 / np.sqrt(F) / s),
            "ffn2_b": bf(np.random.standard_normal(C) * 0.02),
            "scale_ffn": bf(0.1 * (1.0 + 0.1 * np.random.standard_normal(1))),
            "ln2_w": bf(1.0 + 0.1 * np.random.standard_normal(C)),
            "ln2_b": bf(0.1 * np.random.standard_normal(C)),
            "scale_norm2": bf(1.5 * (1.0 + 0.1 * np.random.standard_normal(1))),
            "x": bf(np.random.standard_normal((B, C, HH, WW)))}


def reference(h, ffn2_w, ffn2_b, scale_ffn, ln2_w, ln2_b, scale_norm2, x):
    y2 = ((mxq(f64(h), 3, "e4m3") @ mxq(f64(ffn2_w), 1, "e4m3").T) + f64(ffn2_b)) * f64(scale_ffn)
    y2 = layer_norm(y2, f64(ln2_w), f64(ln2_b)) * f64(scale_norm2)
    out = np.maximum(y2 + f64(x).transpose(0, 2, 3, 1), 0.0)
    return out.transpose(0, 3, 1, 2)

@@ -1,0 +1,273 @@
+from contextlib import ExitStack
+
+import concourse.mybir as mybir
+from concourse.masks import make_identity
+
+F32 = mybir.dt.float32
+BF16 = mybir.dt.bfloat16
+U32 = mybir.dt.uint32
+U8 = mybir.dt.uint8
+FP8X4 = mybir.dt.float8_e4m3fn_x4
+ALU = mybir.AluOpType
+ACT = mybir.ActivationFunctionType
+
+P = 128
+K = 2048
+K_PASS = 512
+PASSES = K // K_PASS
+WORDS_PASS = K_PASS // 2
+CHANNELS = 512
+CH_BLOCKS = CHANNELS // P
+IMAGES = 4
+IMAGE_PIXELS = 256
+TILES = IMAGES * IMAGE_PIXELS // P
+TILES_IMAGE = IMAGE_PIXELS // P
+EPS = 1e-5
+
+AHEAD = 2
+BEHIND = 6
+TURN_BANKS = 6
+
+FLOPS = 2 * IMAGES * IMAGE_PIXELS * CHANNELS * K
+
+
+def tile_transformerconvblock_pc_kernel(
+    tc, h, ffn2_w, ffn2_b, scale_ffn, ln2_w, ln2_b, scale_norm2, x, out
+):
+    nc = tc.nc
+
+    h_rows = h.rearrange("b i j k -> (b i j) k")
+    w_blocks = ffn2_w.rearrange("(r t) k -> r t k", t=CH_BLOCKS)
+    x_images = x.rearrange("b (r t) i j -> r b (t i j)", t=CH_BLOCKS)
+    out_images = out.rearrange("b (r t) i j -> r b (t i j)", t=CH_BLOCKS)
+
+    with ExitStack() as stack:
+        stack.enter_context(tc.manual_schedule())
+        const = stack.enter_context(tc.tile_pool(name="const", bufs=1))
+        raw = stack.enter_context(tc.tile_pool(name="raw", bufs=1))
+        front = stack.enter_context(tc.tile_pool(name="front", bufs=3))
+        back = stack.enter_context(tc.tile_pool(name="back", bufs=3))
+        image = stack.enter_context(tc.tile_pool(name="image", bufs=3))
+        psum = stack.enter_context(tc.psum_pool(name="psum", bufs=2))
+
+        vec_rows = const.tile([P, CHANNELS + 32], BF16)
+        nc.vector.memset(vec_rows[:], 0.0)
+        ones = const.tile([P, P], BF16)
+        nc.vector.memset(ones[:], 1.0)
+        nc.scalar.dma_start(out=vec_rows[0:1, 0:CHANNELS], in_=ffn2_b.rearrange("(o c) -> o c", o=1))
+        nc.scalar.dma_start(
+            out=vec_rows[0:1, CHANNELS : CHANNELS + 1], in_=scale_ffn.rearrange("(o c) -> o c", o=1)
+        )
+        nc.scalar.dma_start(
+            out=vec_rows[0:1, CHANNELS + 16 : CHANNELS + 17],
+            in_=scale_norm2.rearrange("(o c) -> o c", o=1),
+        )
+        gain_raw = const.tile([P, CH_BLOCKS], BF16)
+        nc.scalar.dma_start(out=gain_raw[:], in_=ln2_w.rearrange("(r t) -> r t", t=CH_BLOCKS))
+        shift_raw = const.tile([P, CH_BLOCKS], BF16)
+        nc.scalar.dma_start(out=shift_raw[:], in_=ln2_b.rearrange("(r t) -> r t", t=CH_BLOCKS))
+
+        warm = const.tile([P, 1], F32)
+        nc.scalar.activation(out=warm[:], in_=ones[:, 0:1], func=ACT.Abs_reciprocal_sqrt)
+
+        w_raw = [load_rows(nc, raw, w_blocks[:, t, :], "w_raw%d" % t, 1) for t in range(CH_BLOCKS)]
+        h_raw = []
+        x_raw = []
+        for i in range(TILES):
+            h_raw.append(load_rows(nc, raw, h_rows[i * P : (i + 1) * P, :], "h_raw%d" % i, 2))
+            if i >= TILES_IMAGE and i % TILES_IMAGE == 1:
+                load_x(nc, raw, x_images, x_raw)
+        load_x(nc, raw, x_images, x_raw)
+
+        ident = const.tile([P, P], F32)
+        make_identity(nc, ident[:])
+
+        w_codes = const.tile([P, PASSES, CHANNELS], U32, align_bytes=64)
+        w_scales = const.tile([P, PASSES, CHANNELS], U8, align_bytes=64)
+        for t in range(CH_BLOCKS):
+            w_grouped = front.tile([P, PASSES * P * 4], BF16, tag="grouped", align_bytes=64)
+            k_to_partitions(nc, psum, w_raw[t], ident, w_grouped, (nc.scalar.copy, nc.vector.tensor_copy))
+            for g in range(PASSES):
+                nc.vector.quantize_mx(
+                    out=w_codes[:, g, t * P : (t + 1) * P].bitcast(FP8X4),
+                    scales=w_scales[:, g, t * P : (t + 1) * P],
+                    in_=w_grouped[:, g * P * 4 : (g + 1) * P * 4],
+                )
+
+        bias_all = const.tile([P, CH_BLOCKS, P], F32)
+        mult = const.tile([P, 32], F32)
+        s_ffn = mult[:, 0:1]
+        s_norm = mult[:, 16:17]
+        s_ffn_sq = const.tile([P, 1], F32)
+        eps = const.tile([P, 1], F32)
+        gain = const.tile([P, CH_BLOCKS], F32)
+        shift = const.tile([P, CH_BLOCKS], F32)
+
+        def spread_constants():
+            bias_ps = psum.tile([P, CHANNELS], F32, tag="bank", bufs=TURN_BANKS)
+            nc.tensor.matmul(out=bias_ps[:], lhsT=ones[:], rhs=vec_rows[:, 0:CHANNELS], start=True, stop=True)
+            mult_ps = psum.tile([P, 32], F32, tag="bank", bufs=TURN_BANKS)
+            nc.tensor.matmul(
+                out=mult_ps[:], lhsT=ones[:], rhs=vec_rows[:, CHANNELS : CHANNELS + 32], start=True, stop=True
+            )
+            nc.vector.tensor_copy(out=bias_all[:], in_=bias_ps[:].rearrange("p (r t) -> p t r", t=CH_BLOCKS))
+            nc.vector.tensor_copy(out=mult[:], in_=mult_ps[:])
+            nc.vector.tensor_scalar_mul(out=eps[:], in0=ones[:, 0:1], scalar1=EPS)
+            nc.vector.tensor_scalar_mul(out=shift[:], in0=shift_raw[:], scalar1=s_norm)
+            nc.vector.tensor_scalar(
+                out=gain[:], in0=gain_raw[:], scalar1=s_norm, scalar2=s_ffn, op0=ALU.mult, op1=ALU.mult
+            )
+            nc.vector.tensor_mul(out=s_ffn_sq[:], in0=s_ffn, in1=s_ffn)
+
+        grouped = {}
+        codes = {}
+        scales = {}
+        acc = {}
+        v = {}
+        stats = {}
+        normed = {}
+        turned = {}
+
+        def transpose_h(i):
+            grouped[i] = front.tile([P, PASSES * P * 4], BF16, tag="grouped", name="h_grouped", align_bytes=64)
+            k_to_partitions(nc, psum, h_raw[i], ident, grouped[i], (nc.scalar.copy, nc.scalar.copy))
+
+        def quantise_h(i):
+            codes[i] = front.tile([P, PASSES * P], U32, tag="codes", name="h_codes", align_bytes=64)
+            scales[i] = front.tile([P, PASSES * P], U8, tag="scales", name="h_scales", align_bytes=64)
+            for half in range(2):
+                nc.vector.quantize_mx(
+                    out=codes[i][:, half * 2 * P : (half + 1) * 2 * P].bitcast(FP8X4),
+                    scales=scales[i][:, half * 2 * P : (half + 1) * 2 * P],
+                    in_=grouped[i][:, half * 8 * P : (half + 1) * 8 * P],
+                )
+
+        def multiply(i):
+            acc[i] = psum.tile([P, CHANNELS], F32, tag="acc", name="acc")
+            for g in range(PASSES):
+                nc.tensor.matmul_mx(
+                    out=acc[i][:],
+                    lhsT=codes[i][:, g * P : (g + 1) * P].bitcast(FP8X4),
+                    lhsT_scale=scales[i][:, g * P : (g + 1) * P],
+                    rhs=w_codes[:, g, :].bitcast(FP8X4),
+                    rhs_scale=w_scales[:, g, :],
+                    start=(g == 0),
+                    stop=(g == PASSES - 1),
+                )
+
+        def add_bias(i):
+            v[i] = back.tile([P, CHANNELS], F32, tag="v", name="v")
+            nc.vector.tensor_tensor(
+                out=v[i][:], in0=acc[i][:], in1=bias_all[:].rearrange("p t r -> p (t r)"), op=ALU.add
+            )
+
+        def sum_up(i):
+            stats[i] = back.tile([P, 6], F32, tag="stats", name="stats")
+            nc.vector.bn_stats(out=stats[i][:], in_=v[i][:])
+
+        def normalise(i):
+            moments = back.tile([P, 2], F32, tag="moments")
+            nc.vector.bn_aggr(out=moments[:], in_=stats[i][:])
+            neg_mean = back.tile([P, 1], F32, tag="neg_mean")
+            nc.gpsimd.tensor_scalar(
+                out=neg_mean[:], in0=moments[:, 0:1], scalar1=-1.0, scalar2=0.0, op0=ALU.mult, op1=ALU.add
+            )
+            inv_std = back.tile([P, 1], F32, tag="inv_std")
+            nc.scalar.activation(
+                out=inv_std[:], in_=moments[:, 1:2], func=ACT.Abs_reciprocal_sqrt, bias=eps[:], scale=s_ffn_sq[:]
+            )
+            normed[i] = back.tile([P, CHANNELS], F32, tag="normed", name="normed", bufs=BEHIND + 1)
+            nc.gpsimd.tensor_scalar(
+                out=normed[i][:], in0=v[i][:], scalar1=neg_mean[:], scalar2=inv_std[:], op0=ALU.add, op1=ALU.mult
+            )
+
+        def turn_back(b):
+            turned[b] = [
+                psum.tile([P, 2, IMAGE_PIXELS], F32, tag="bank", name="turned%d" % half, bufs=TURN_BANKS)
+                for half in range(2)
+            ]
+            for part in range(TILES_IMAGE):
+                for t in range(CH_BLOCKS):
+                    nc.tensor.transpose(
+                        turned[b][t // 2][:, t % 2, part * P : (part + 1) * P],
+                        normed[b * TILES_IMAGE + part][:, t * P : (t + 1) * P],
+                        ident[:],
+                    )
+
+        def finish(b):
+            summed = image.tile([P, CH_BLOCKS, IMAGE_PIXELS], F32, tag="summed")
+            result = image.tile([P, CH_BLOCKS, IMAGE_PIXELS], F32, tag="result")
+            for t in range(CH_BLOCKS):
+                nc.vector.scalar_tensor_tensor(
+                    out=summed[:, t, :],
+                    in0=turned[b][t // 2][:, t % 2, :],
+                    scalar=gain[:, t : t + 1],
+                    in1=x_raw[b][:, t * IMAGE_PIXELS : (t + 1) * IMAGE_PIXELS],
+                    op0=ALU.mult,
+                    op1=ALU.add,
+                )
+            for t in range(CH_BLOCKS):
+                nc.scalar.activation(
+                    out=result[:, t, :], in_=summed[:, t, :], func=ACT.Relu, bias=shift[:, t : t + 1], scale=1.0
+                )
+                nc.sync.dma_start(
+                    out=out_images[:, b, t * IMAGE_PIXELS : (t + 1) * IMAGE_PIXELS], in_=result[:, t, :]
+                )
+
+        transpose_h(0)
+        quantise_h(0)
+        spread_constants()
+        for i in range(1, AHEAD):
+            transpose_h(i)
+            quantise_h(i)
+        for i in range(TILES + BEHIND):
+            image_done = (i - BEHIND) // TILES_IMAGE if (i - BEHIND) % TILES_IMAGE == 0 else -1
+            if i < TILES:
+                multiply(i)
+            if i + AHEAD < TILES:
+                transpose_h(i + AHEAD)
+            if 0 <= image_done < IMAGES:
+                turn_back(image_done)
+            if i < TILES:
+                add_bias(i)
+            if 0 <= i - 1 < TILES:
+                normalise(i - 1)
+            if 0 <= image_done < IMAGES:
+                finish(image_done)
+            if i + AHEAD < TILES:
+                quantise_h(i + AHEAD)
+            if i < TILES:
+                sum_up(i)
+
+
+def load_rows(nc, pool, rows, name, pieces):
+    width = K // pieces
+    halves = []
+    for piece in range(pieces):
+        part = pool.tile([P, width], BF16, name="%s_%d" % (name, piece))
+        nc.sync.dma_start(out=part[:], in_=rows[:, piece * width : (piece + 1) * width])
+        for j in range(2 // pieces):
+            halves.append(part[:, j * (K // 2) : (j + 1) * (K // 2)])
+    return halves
+
+
+def load_x(nc, pool, x_images, x_raw):
+    b = len(x_raw)
+    x_tile = pool.tile([P, CH_BLOCKS * IMAGE_PIXELS], BF16, name="x_raw%d" % b)
+    nc.sync.dma_start(out=x_tile[:], in_=x_images[:, b, :])
+    x_raw.append(x_tile)
+
+
+def k_to_partitions(nc, psum, rows, ident, grouped, copiers):
+    grouped_words = grouped[:].bitcast(F32).rearrange("p (g r u) -> p g r u", g=PASSES, u=2)
+    for half in range(2):
+        words = rows[half].bitcast(F32)
+        bank = psum.tile([P, 2, 2, P], F32, tag="bank", bufs=TURN_BANKS)
+        for g in range(2):
+            for u in range(2):
+                nc.tensor.transpose(
+                    bank[:, g, u, :], words[:, g * WORDS_PASS + u : (g + 1) * WORDS_PASS : 2], ident[:]
+                )
+        copiers[half](
+            out=grouped_words[:, 2 * half : 2 * half + 2, :, :], in_=bank[:].rearrange("p g u r -> p g r u")
+        )

@@ -25,7 +25,7 @@ TILES_IMAGE = IMAGE_PIXELS // P
 EPS = 1e-5
 
 AHEAD = 2
-BEHIND = 6
+BEHIND = 5
 TURN_BANKS = 6
 
 FLOPS = 2 * IMAGES * IMAGE_PIXELS * CHANNELS * K
@@ -85,8 +85,9 @@ def tile_transformerconvblock_pc_kernel(
         w_codes = const.tile([P, PASSES, CHANNELS], U32, align_bytes=64)
         w_scales = const.tile([P, PASSES, CHANNELS], U8, align_bytes=64)
         for t in range(CH_BLOCKS):
-            w_grouped = front.tile([P, PASSES * P * 4], BF16, tag="grouped", align_bytes=64)
-            k_to_partitions(nc, psum, w_raw[t], ident, w_grouped, (nc.scalar.copy, nc.vector.tensor_copy))
+            w_grouped = front.tile([P, PASSES * P * 4], BF16, tag="w_grouped", align_bytes=64)
+            second_copier = nc.vector.tensor_copy if t % 2 == 1 else nc.scalar.copy
+            k_to_partitions(nc, psum, w_raw[t], ident, w_grouped, (nc.scalar.copy, second_copier))
             for g in range(PASSES):
                 nc.vector.quantize_mx(
                     out=w_codes[:, g, t * P : (t + 1) * P].bitcast(FP8X4),
@@ -99,6 +100,7 @@ def tile_transformerconvblock_pc_kernel(
         s_ffn = mult[:, 0:1]
         s_norm = mult[:, 16:17]
         s_ffn_sq = const.tile([P, 1], F32)
+        s_ffn_sq_mean = const.tile([P, 1], F32)
         eps = const.tile([P, 1], F32)
         gain = const.tile([P, CH_BLOCKS], F32)
         shift = const.tile([P, CH_BLOCKS], F32)
@@ -118,6 +120,10 @@ def tile_transformerconvblock_pc_kernel(
                 out=gain[:], in0=gain_raw[:], scalar1=s_norm, scalar2=s_ffn, op0=ALU.mult, op1=ALU.mult
             )
             nc.vector.tensor_mul(out=s_ffn_sq[:], in0=s_ffn, in1=s_ffn)
+            nc.vector.tensor_scalar_mul(out=s_ffn_sq_mean[:], in0=s_ffn_sq[:], scalar1=1.0 / CHANNELS)
+
+        def squares_on_scalar(i):
+            return i % 3 == 0
 
         grouped = {}
         codes = {}
@@ -125,6 +131,10 @@ def tile_transformerconvblock_pc_kernel(
         acc = {}
         v = {}
         stats = {}
+        sums = {}
+        mean = {}
+        neg_mean = {}
+        inv_std = {}
         normed = {}
         turned = {}
 
@@ -133,8 +143,8 @@ def tile_transformerconvblock_pc_kernel(
             k_to_partitions(nc, psum, h_raw[i], ident, grouped[i], (nc.scalar.copy, nc.scalar.copy))
 
         def quantise_h(i):
-            codes[i] = front.tile([P, PASSES * P], U32, tag="codes", name="h_codes", align_bytes=64)
-            scales[i] = front.tile([P, PASSES * P], U8, tag="scales", name="h_scales", align_bytes=64)
+            codes[i] = front.tile([P, PASSES * P], U32, tag="codes", name="h_codes", align_bytes=64, bufs=4)
+            scales[i] = front.tile([P, PASSES * P], U8, tag="scales", name="h_scales", align_bytes=64, bufs=4)
             for half in range(2):
                 nc.vector.quantize_mx(
                     out=codes[i][:, half * 2 * P : (half + 1) * 2 * P].bitcast(FP8X4),
@@ -156,30 +166,62 @@ def tile_transformerconvblock_pc_kernel(
                 )
 
         def add_bias(i):
-            v[i] = back.tile([P, CHANNELS], F32, tag="v", name="v")
-            nc.vector.tensor_tensor(
-                out=v[i][:], in0=acc[i][:], in1=bias_all[:].rearrange("p t r -> p (t r)"), op=ALU.add
-            )
+            v[i] = back.tile([P, CHANNELS], F32, tag="v", name="v", bufs=4)
+            bias_row = bias_all[:].rearrange("p t r -> p (t r)")
+            if squares_on_scalar(i):
+                sums[i] = back.tile([P, 1], F32, tag="sums", name="sums", bufs=4)
+                nc.vector.scalar_tensor_tensor(
+                    out=v[i][:],
+                    in0=acc[i][:],
+                    scalar=1.0,
+                    in1=bias_row,
+                    op0=ALU.mult,
+                    op1=ALU.add,
+                    accum_out=sums[i][:],
+                )
+            else:
+                nc.vector.tensor_tensor(out=v[i][:], in0=acc[i][:], in1=bias_row, op=ALU.add)
 
         def sum_up(i):
-            stats[i] = back.tile([P, 6], F32, tag="stats", name="stats")
-            nc.vector.bn_stats(out=stats[i][:], in_=v[i][:])
+            if not squares_on_scalar(i):
+                stats[i] = back.tile([P, 6], F32, tag="stats", name="stats", bufs=4)
+                nc.vector.bn_stats(out=stats[i][:], in_=v[i][:])
+
+        def find_spread(i):
+            neg_mean[i] = back.tile([P, 1], F32, tag="neg_mean", name="neg_mean", bufs=4)
+            inv_std[i] = back.tile([P, 1], F32, tag="inv_std", name="inv_std", bufs=4)
+            if squares_on_scalar(i):
+                nc.scalar.activation(out=neg_mean[i][:], in_=sums[i][:], func=ACT.Copy, scale=-1.0 / CHANNELS)
+                squares = back.tile([P, CHANNELS], F32, tag="squares")
+                square_sum = back.tile([P, 1], F32, tag="square_sum")
+                nc.scalar.activation(
+                    out=squares[:], in_=v[i][:], func=ACT.Square, bias=neg_mean[i][:], accum_out=square_sum[:]
+                )
+                variance, scale = square_sum[:], s_ffn_sq_mean[:]
+            else:
+                moments = back.tile([P, 2], F32, tag="moments")
+                nc.vector.bn_aggr(out=moments[:], in_=stats[i][:])
+                if i == TILES - 1:
+                    mean[i] = moments[:, 0:1]
+                else:
+                    nc.gpsimd.tensor_scalar(
+                        out=neg_mean[i][:], in0=moments[:, 0:1], scalar1=-1.0, scalar2=0.0, op0=ALU.mult, op1=ALU.add
+                    )
+                variance, scale = moments[:, 1:2], s_ffn_sq[:]
+            nc.scalar.activation(
+                out=inv_std[i][:], in_=variance, func=ACT.Abs_reciprocal_sqrt, bias=eps[:], scale=scale
+            )
 
         def normalise(i):
-            moments = back.tile([P, 2], F32, tag="moments")
-            nc.vector.bn_aggr(out=moments[:], in_=stats[i][:])
-            neg_mean = back.tile([P, 1], F32, tag="neg_mean")
-            nc.gpsimd.tensor_scalar(
-                out=neg_mean[:], in0=moments[:, 0:1], scalar1=-1.0, scalar2=0.0, op0=ALU.mult, op1=ALU.add
-            )
-            inv_std = back.tile([P, 1], F32, tag="inv_std")
-            nc.scalar.activation(
-                out=inv_std[:], in_=moments[:, 1:2], func=ACT.Abs_reciprocal_sqrt, bias=eps[:], scale=s_ffn_sq[:]
-            )
             normed[i] = back.tile([P, CHANNELS], F32, tag="normed", name="normed", bufs=BEHIND + 1)
-            nc.gpsimd.tensor_scalar(
-                out=normed[i][:], in0=v[i][:], scalar1=neg_mean[:], scalar2=inv_std[:], op0=ALU.add, op1=ALU.mult
-            )
+            if i == TILES - 1:
+                nc.vector.tensor_scalar(
+                    out=normed[i][:], in0=v[i][:], scalar1=mean[i], scalar2=inv_std[i][:], op0=ALU.subtract, op1=ALU.mult
+                )
+            else:
+                nc.gpsimd.tensor_scalar(
+                    out=normed[i][:], in0=v[i][:], scalar1=neg_mean[i][:], scalar2=inv_std[i][:], op0=ALU.add, op1=ALU.mult
+                )
 
         def turn_back(b):
             turned[b] = [
@@ -194,24 +236,25 @@ def tile_transformerconvblock_pc_kernel(
                         ident[:],
                     )
 
-        def finish(b):
-            summed = image.tile([P, CH_BLOCKS, IMAGE_PIXELS], F32, tag="summed")
-            result = image.tile([P, CH_BLOCKS, IMAGE_PIXELS], F32, tag="result")
-            for t in range(CH_BLOCKS):
+        def finish(b, half):
+            blocks = (2 * half, 2 * half + 1)
+            summed = image.tile([P, 2, IMAGE_PIXELS], F32, tag="summed", bufs=6)
+            result = image.tile([P, 2, IMAGE_PIXELS], F32, tag="result", bufs=6)
+            for j, t in enumerate(blocks):
                 nc.vector.scalar_tensor_tensor(
-                    out=summed[:, t, :],
+                    out=summed[:, j, :],
                     in0=turned[b][t // 2][:, t % 2, :],
                     scalar=gain[:, t : t + 1],
                     in1=x_raw[b][:, t * IMAGE_PIXELS : (t + 1) * IMAGE_PIXELS],
                     op0=ALU.mult,
                     op1=ALU.add,
                 )
-            for t in range(CH_BLOCKS):
+            for j, t in enumerate(blocks):
                 nc.scalar.activation(
-                    out=result[:, t, :], in_=summed[:, t, :], func=ACT.Relu, bias=shift[:, t : t + 1], scale=1.0
+                    out=result[:, j, :], in_=summed[:, j, :], func=ACT.Relu, bias=shift[:, t : t + 1], scale=1.0
                 )
                 nc.sync.dma_start(
-                    out=out_images[:, b, t * IMAGE_PIXELS : (t + 1) * IMAGE_PIXELS], in_=result[:, t, :]
+                    out=out_images[:, b, t * IMAGE_PIXELS : (t + 1) * IMAGE_PIXELS], in_=result[:, j, :]
                 )
 
         transpose_h(0)
@@ -221,23 +264,30 @@ def tile_transformerconvblock_pc_kernel(
             transpose_h(i)
             quantise_h(i)
         for i in range(TILES + BEHIND):
-            image_done = (i - BEHIND) // TILES_IMAGE if (i - BEHIND) % TILES_IMAGE == 0 else -1
+            turned_now = i - BEHIND if 0 <= i - BEHIND < TILES and (i - BEHIND) % TILES_IMAGE == 0 else None
             if i < TILES:
                 multiply(i)
             if i + AHEAD < TILES:
                 transpose_h(i + AHEAD)
-            if 0 <= image_done < IMAGES:
-                turn_back(image_done)
+            if turned_now is not None:
+                turn_back(turned_now // TILES_IMAGE)
             if i < TILES:
                 add_bias(i)
             if 0 <= i - 1 < TILES:
-                normalise(i - 1)
-            if 0 <= image_done < IMAGES:
-                finish(image_done)
-            if i + AHEAD < TILES:
-                quantise_h(i + AHEAD)
+                find_spread(i - 1)
             if i < TILES:
                 sum_up(i)
+            if 0 <= i - BEHIND < TILES:
+                b, half = (i - BEHIND) // 2, (i - BEHIND) % 2
+                if b < IMAGES - 2:
+                    finish(b, half)
+                elif half == 0:
+                    finish(b, 0)
+                    finish(b, 1)
+            if 0 <= i - 1 < TILES:
+                normalise(i - 1)
+            if i + AHEAD < TILES:
+                quantise_h(i + AHEAD)
 
 
 def load_rows(nc, pool, rows, name, pieces):

@@ -26,6 +26,7 @@ EPS = 1e-5
 
 AHEAD = 2
 BEHIND = 5
+ORDERED = (2, 3, 4)
 TURN_BANKS = 6
 
 FLOPS = 2 * IMAGES * IMAGE_PIXELS * CHANNELS * K
@@ -87,7 +88,8 @@ def tile_transformerconvblock_pc_kernel(
         for t in range(CH_BLOCKS):
             w_grouped = front.tile([P, PASSES * P * 4], BF16, tag="w_grouped", align_bytes=64)
             second_copier = nc.vector.tensor_copy if t % 2 == 1 else nc.scalar.copy
-            k_to_partitions(nc, psum, w_raw[t], ident, w_grouped, (nc.scalar.copy, second_copier))
+            columns = [every_second_word(part) for part in w_raw[t]]
+            k_to_partitions(nc, psum, columns, ident, w_grouped, (nc.scalar.copy, second_copier))
             for g in range(PASSES):
                 nc.vector.quantize_mx(
                     out=w_codes[:, g, t * P : (t + 1) * P].bitcast(FP8X4),
@@ -138,9 +140,25 @@ def tile_transformerconvblock_pc_kernel(
         normed = {}
         turned = {}
 
+        ordered = {}
+
+        def order_words(i):
+            ordered[i] = []
+            for half in range(2):
+                words = front.tile([P, 2, 2, P], F32, tag="ordered", name="ordered", bufs=6)
+                nc.vector.tensor_copy(
+                    out=words[:], in_=h_raw[i][half].bitcast(F32).rearrange("r (g p u) -> r g u p", g=2, u=2)
+                )
+                ordered[i].append(words)
+
         def transpose_h(i):
             grouped[i] = front.tile([P, PASSES * P * 4], BF16, tag="grouped", name="h_grouped", align_bytes=64)
-            k_to_partitions(nc, psum, h_raw[i], ident, grouped[i], (nc.scalar.copy, nc.scalar.copy))
+            copiers = (nc.scalar.copy, nc.scalar.copy)
+            if i in ORDERED:
+                columns = [[[words[:, g, u, :] for u in range(2)] for g in range(2)] for words in ordered[i]]
+            else:
+                columns = [every_second_word(part) for part in h_raw[i]]
+            k_to_partitions(nc, psum, columns, ident, grouped[i], copiers)
 
         def quantise_h(i):
             codes[i] = front.tile([P, PASSES * P], U32, tag="codes", name="h_codes", align_bytes=64, bufs=4)
@@ -262,6 +280,7 @@ def tile_transformerconvblock_pc_kernel(
         spread_constants()
         for i in range(1, AHEAD):
             transpose_h(i)
+            order_words(i + 1)
             quantise_h(i)
         for i in range(TILES + BEHIND):
             turned_now = i - BEHIND if 0 <= i - BEHIND < TILES and (i - BEHIND) % TILES_IMAGE == 0 else None
@@ -271,6 +290,8 @@ def tile_transformerconvblock_pc_kernel(
                 transpose_h(i + AHEAD)
             if turned_now is not None:
                 turn_back(turned_now // TILES_IMAGE)
+            if i + AHEAD + 1 in ORDERED:
+                order_words(i + AHEAD + 1)
             if i < TILES:
                 add_bias(i)
             if 0 <= i - 1 < TILES:
@@ -308,16 +329,18 @@ def load_x(nc, pool, x_images, x_raw):
     x_raw.append(x_tile)
 
 
-def k_to_partitions(nc, psum, rows, ident, grouped, copiers):
+def every_second_word(rows):
+    words = rows.bitcast(F32)
+    return [[words[:, g * WORDS_PASS + u : (g + 1) * WORDS_PASS : 2] for u in range(2)] for g in range(2)]
+
+
+def k_to_partitions(nc, psum, columns, ident, grouped, copiers):
     grouped_words = grouped[:].bitcast(F32).rearrange("p (g r u) -> p g r u", g=PASSES, u=2)
     for half in range(2):
-        words = rows[half].bitcast(F32)
         bank = psum.tile([P, 2, 2, P], F32, tag="bank", bufs=TURN_BANKS)
         for g in range(2):
             for u in range(2):
-                nc.tensor.transpose(
-                    bank[:, g, u, :], words[:, g * WORDS_PASS + u : (g + 1) * WORDS_PASS : 2], ident[:]
-                )
+                nc.tensor.transpose(bank[:, g, u, :], columns[half][g][u], ident[:])
         copiers[half](
             out=grouped_words[:, 2 * half : 2 * half + 2, :, :], in_=bank[:].rearrange("p g u r -> p g r u")
         )

@@ -25,8 +25,7 @@ TILES_IMAGE = IMAGE_PIXELS // P
 EPS = 1e-5
 
 AHEAD = 2
-BEHIND = 5
-ORDERED = (2, 3, 4)
+ORDERED = (2, 4)
 TURN_BANKS = 6
 
 FLOPS = 2 * IMAGES * IMAGE_PIXELS * CHANNELS * K
@@ -102,7 +101,7 @@ def tile_transformerconvblock_pc_kernel(
         s_ffn = mult[:, 0:1]
         s_norm = mult[:, 16:17]
         s_ffn_sq = const.tile([P, 1], F32)
-        s_ffn_sq_mean = const.tile([P, 1], F32)
+        s_ffn_sq_cube = const.tile([P, 1], F32)
         eps = const.tile([P, 1], F32)
         gain = const.tile([P, CH_BLOCKS], F32)
         shift = const.tile([P, CH_BLOCKS], F32)
@@ -114,18 +113,18 @@ def tile_transformerconvblock_pc_kernel(
             nc.tensor.matmul(
                 out=mult_ps[:], lhsT=ones[:], rhs=vec_rows[:, CHANNELS : CHANNELS + 32], start=True, stop=True
             )
-            nc.vector.tensor_copy(out=bias_all[:], in_=bias_ps[:].rearrange("p (r t) -> p t r", t=CH_BLOCKS))
-            nc.vector.tensor_copy(out=mult[:], in_=mult_ps[:])
-            nc.vector.tensor_scalar_mul(out=eps[:], in0=ones[:, 0:1], scalar1=EPS)
-            nc.vector.tensor_scalar_mul(out=shift[:], in0=shift_raw[:], scalar1=s_norm)
-            nc.vector.tensor_scalar(
+            nc.scalar.copy(out=bias_all[:], in_=bias_ps[:].rearrange("p (r t) -> p t r", t=CH_BLOCKS))
+            nc.scalar.copy(out=mult[:], in_=mult_ps[:])
+            nc.gpsimd.tensor_mul(out=s_ffn_sq[:], in0=s_ffn, in1=s_ffn)
+            nc.gpsimd.tensor_scalar_mul(out=s_ffn_sq_cube[:], in0=s_ffn_sq[:], scalar1=1.0 / CHANNELS**3)
+            nc.gpsimd.tensor_scalar_mul(out=eps[:], in0=ones[:, 0:1], scalar1=EPS)
+            nc.gpsimd.tensor_scalar_mul(out=shift[:], in0=shift_raw[:], scalar1=s_norm)
+            nc.gpsimd.tensor_scalar(
                 out=gain[:], in0=gain_raw[:], scalar1=s_norm, scalar2=s_ffn, op0=ALU.mult, op1=ALU.mult
             )
-            nc.vector.tensor_mul(out=s_ffn_sq[:], in0=s_ffn, in1=s_ffn)
-            nc.vector.tensor_scalar_mul(out=s_ffn_sq_mean[:], in0=s_ffn_sq[:], scalar1=1.0 / CHANNELS)
 
         def squares_on_scalar(i):
-            return i % 3 == 0
+            return i % 4 != 3
 
         grouped = {}
         codes = {}
@@ -135,6 +134,7 @@ def tile_transformerconvblock_pc_kernel(
         stats = {}
         sums = {}
         mean = {}
+        variance = {}
         neg_mean = {}
         inv_std = {}
         normed = {}
@@ -207,31 +207,39 @@ def tile_transformerconvblock_pc_kernel(
 
         def find_spread(i):
             neg_mean[i] = back.tile([P, 1], F32, tag="neg_mean", name="neg_mean", bufs=4)
-            inv_std[i] = back.tile([P, 1], F32, tag="inv_std", name="inv_std", bufs=4)
             if squares_on_scalar(i):
-                nc.scalar.activation(out=neg_mean[i][:], in_=sums[i][:], func=ACT.Copy, scale=-1.0 / CHANNELS)
                 squares = back.tile([P, CHANNELS], F32, tag="squares")
-                square_sum = back.tile([P, 1], F32, tag="square_sum")
+                square_sum = back.tile([P, 1], F32, tag="square_sum", bufs=4)
                 nc.scalar.activation(
-                    out=squares[:], in_=v[i][:], func=ACT.Square, bias=neg_mean[i][:], accum_out=square_sum[:]
+                    out=squares[:],
+                    in_=v[i][:],
+                    func=ACT.Square,
+                    bias=sums[i][:],
+                    scale=-float(CHANNELS),
+                    accum_out=square_sum[:],
                 )
-                variance, scale = square_sum[:], s_ffn_sq_mean[:]
+                variance[i] = (square_sum[:], s_ffn_sq_cube[:])
+                nc.gpsimd.tensor_scalar(
+                    out=neg_mean[i][:], in0=sums[i][:], scalar1=-1.0 / CHANNELS, scalar2=0.0, op0=ALU.mult, op1=ALU.add
+                )
             else:
-                moments = back.tile([P, 2], F32, tag="moments")
+                moments = back.tile([P, 2], F32, tag="moments", bufs=4)
                 nc.vector.bn_aggr(out=moments[:], in_=stats[i][:])
+                variance[i] = (moments[:, 1:2], s_ffn_sq[:])
                 if i == TILES - 1:
                     mean[i] = moments[:, 0:1]
                 else:
                     nc.gpsimd.tensor_scalar(
                         out=neg_mean[i][:], in0=moments[:, 0:1], scalar1=-1.0, scalar2=0.0, op0=ALU.mult, op1=ALU.add
                     )
-                variance, scale = moments[:, 1:2], s_ffn_sq[:]
-            nc.scalar.activation(
-                out=inv_std[i][:], in_=variance, func=ACT.Abs_reciprocal_sqrt, bias=eps[:], scale=scale
-            )
+
+        def invert(i):
+            inv_std[i] = back.tile([P, 1], F32, tag="inv_std", name="inv_std", bufs=4)
+            spread, scale = variance[i]
+            nc.scalar.activation(out=inv_std[i][:], in_=spread, func=ACT.Abs_reciprocal_sqrt, bias=eps[:], scale=scale)
 
         def normalise(i):
-            normed[i] = back.tile([P, CHANNELS], F32, tag="normed", name="normed", bufs=BEHIND + 1)
+            normed[i] = back.tile([P, CHANNELS], F32, tag="normed", name="normed", bufs=6)
             if i == TILES - 1:
                 nc.vector.tensor_scalar(
                     out=normed[i][:], in0=v[i][:], scalar1=mean[i], scalar2=inv_std[i][:], op0=ALU.subtract, op1=ALU.mult
@@ -278,37 +286,35 @@ def tile_transformerconvblock_pc_kernel(
         transpose_h(0)
         quantise_h(0)
         spread_constants()
-        for i in range(1, AHEAD):
-            transpose_h(i)
-            order_words(i + 1)
-            quantise_h(i)
-        for i in range(TILES + BEHIND):
-            turned_now = i - BEHIND if 0 <= i - BEHIND < TILES and (i - BEHIND) % TILES_IMAGE == 0 else None
+        order_words(2)
+        transpose_h(1)
+        quantise_h(1)
+        turned_in = {min(2 * b + 5, b + 6): b for b in range(IMAGES)}
+        for i in range(TILES + 3):
             if i < TILES:
                 multiply(i)
+            if 0 <= i - 2 < TILES:
+                normalise(i - 2)
+            if i + 3 in ORDERED:
+                order_words(i + 3)
             if i + AHEAD < TILES:
                 transpose_h(i + AHEAD)
-            if turned_now is not None:
-                turn_back(turned_now // TILES_IMAGE)
-            if i + AHEAD + 1 in ORDERED:
-                order_words(i + AHEAD + 1)
+            if 0 <= i - 1 < TILES:
+                invert(i - 1)
+            if i in turned_in:
+                turn_back(turned_in[i])
+            if i - 1 in turned_in:
+                finish(turned_in[i - 1], 1)
             if i < TILES:
                 add_bias(i)
-            if 0 <= i - 1 < TILES:
-                find_spread(i - 1)
+            if i in turned_in:
+                finish(turned_in[i], 0)
             if i < TILES:
                 sum_up(i)
-            if 0 <= i - BEHIND < TILES:
-                b, half = (i - BEHIND) // 2, (i - BEHIND) % 2
-                if b < IMAGES - 2:
-                    finish(b, half)
-                elif half == 0:
-                    finish(b, 0)
-                    finish(b, 1)
-            if 0 <= i - 1 < TILES:
-                normalise(i - 1)
             if i + AHEAD < TILES:
                 quantise_h(i + AHEAD)
+            if i < TILES:
+                find_spread(i)
 
 
 def load_rows(nc, pool, rows, name, pieces):

from contextlib import ExitStack

import concourse.mybir as mybir
from concourse.masks import make_identity

F32 = mybir.dt.float32
BF16 = mybir.dt.bfloat16
U32 = mybir.dt.uint32
U8 = mybir.dt.uint8
FP8X4 = mybir.dt.float8_e4m3fn_x4
ALU = mybir.AluOpType
ACT = mybir.ActivationFunctionType

P = 128
K = 2048
K_PASS = 512
PASSES = K // K_PASS
WORDS_PASS = K_PASS // 2
CHANNELS = 512
CH_BLOCKS = CHANNELS // P
IMAGES = 4
IMAGE_PIXELS = 256
TILES = IMAGES * IMAGE_PIXELS // P
TILES_IMAGE = IMAGE_PIXELS // P
EPS = 1e-5

AHEAD = 2
ORDERED = (2, 4)
TURN_BANKS = 6

FLOPS = 2 * IMAGES * IMAGE_PIXELS * CHANNELS * K


def tile_transformerconvblock_pc_kernel(
    tc, h, ffn2_w, ffn2_b, scale_ffn, ln2_w, ln2_b, scale_norm2, x, out
):
    nc = tc.nc

    h_rows = h.rearrange("b i j k -> (b i j) k")
    w_blocks = ffn2_w.rearrange("(r t) k -> r t k", t=CH_BLOCKS)
    x_images = x.rearrange("b (r t) i j -> r b (t i j)", t=CH_BLOCKS)
    out_images = out.rearrange("b (r t) i j -> r b (t i j)", t=CH_BLOCKS)

    with ExitStack() as stack:
        stack.enter_context(tc.manual_schedule())
        const = stack.enter_context(tc.tile_pool(name="const", bufs=1))
        raw = stack.enter_context(tc.tile_pool(name="raw", bufs=1))
        front = stack.enter_context(tc.tile_pool(name="front", bufs=3))
        back = stack.enter_context(tc.tile_pool(name="back", bufs=3))
        image = stack.enter_context(tc.tile_pool(name="image", bufs=3))
        psum = stack.enter_context(tc.psum_pool(name="psum", bufs=2))

        vec_rows = const.tile([P, CHANNELS + 32], BF16)
        nc.vector.memset(vec_rows[:], 0.0)
        ones = const.tile([P, P], BF16)
        nc.vector.memset(ones[:], 1.0)
        nc.scalar.dma_start(out=vec_rows[0:1, 0:CHANNELS], in_=ffn2_b.rearrange("(o c) -> o c", o=1))
        nc.scalar.dma_start(
            out=vec_rows[0:1, CHANNELS : CHANNELS + 1], in_=scale_ffn.rearrange("(o c) -> o c", o=1)
        )
        nc.scalar.dma_start(
            out=vec_rows[0:1, CHANNELS + 16 : CHANNELS + 17],
            in_=scale_norm2.rearrange("(o c) -> o c", o=1),
        )
        gain_raw = const.tile([P, CH_BLOCKS], BF16)
        nc.scalar.dma_start(out=gain_raw[:], in_=ln2_w.rearrange("(r t) -> r t", t=CH_BLOCKS))
        shift_raw = const.tile([P, CH_BLOCKS], BF16)
        nc.scalar.dma_start(out=shift_raw[:], in_=ln2_b.rearrange("(r t) -> r t", t=CH_BLOCKS))

        warm = const.tile([P, 1], F32)
        nc.scalar.activation(out=warm[:], in_=ones[:, 0:1], func=ACT.Abs_reciprocal_sqrt)

        w_raw = [load_rows(nc, raw, w_blocks[:, t, :], "w_raw%d" % t, 1) for t in range(CH_BLOCKS)]
        h_raw = []
        x_raw = []
        for i in range(TILES):
            h_raw.append(load_rows(nc, raw, h_rows[i * P : (i + 1) * P, :], "h_raw%d" % i, 2))
            if i >= TILES_IMAGE and i % TILES_IMAGE == 1:
                load_x(nc, raw, x_images, x_raw)
        load_x(nc, raw, x_images, x_raw)

        ident = const.tile([P, P], F32)
        make_identity(nc, ident[:])

        w_codes = const.tile([P, PASSES, CHANNELS], U32, align_bytes=64)
        w_scales = const.tile([P, PASSES, CHANNELS], U8, align_bytes=64)
        for t in range(CH_BLOCKS):
            w_grouped = front.tile([P, PASSES * P * 4], BF16, tag="w_grouped", align_bytes=64)
            second_copier = nc.vector.tensor_copy if t % 2 == 1 else nc.scalar.copy
            columns = [every_second_word(part) for part in w_raw[t]]
            k_to_partitions(nc, psum, columns, ident, w_grouped, (nc.scalar.copy, second_copier))
            for g in range(PASSES):
                nc.vector.quantize_mx(
                    out=w_codes[:, g, t * P : (t + 1) * P].bitcast(FP8X4),
                    scales=w_scales[:, g, t * P : (t + 1) * P],
                    in_=w_grouped[:, g * P * 4 : (g + 1) * P * 4],
                )

        bias_all = const.tile([P, CH_BLOCKS, P], F32)
        mult = const.tile([P, 32], F32)
        s_ffn = mult[:, 0:1]
        s_norm = mult[:, 16:17]
        s_ffn_sq = const.tile([P, 1], F32)
        s_ffn_sq_cube = const.tile([P, 1], F32)
        eps = const.tile([P, 1], F32)
        gain = const.tile([P, CH_BLOCKS], F32)
        shift = const.tile([P, CH_BLOCKS], F32)

        def spread_constants():
            bias_ps = psum.tile([P, CHANNELS], F32, tag="bank", bufs=TURN_BANKS)
            nc.tensor.matmul(out=bias_ps[:], lhsT=ones[:], rhs=vec_rows[:, 0:CHANNELS], start=True, stop=True)
            mult_ps = psum.tile([P, 32], F32, tag="bank", bufs=TURN_BANKS)
            nc.tensor.matmul(
                out=mult_ps[:], lhsT=ones[:], rhs=vec_rows[:, CHANNELS : CHANNELS + 32], start=True, stop=True
            )
            nc.scalar.copy(out=bias_all[:], in_=bias_ps[:].rearrange("p (r t) -> p t r", t=CH_BLOCKS))
            nc.scalar.copy(out=mult[:], in_=mult_ps[:])
            nc.gpsimd.tensor_mul(out=s_ffn_sq[:], in0=s_ffn, in1=s_ffn)
            nc.gpsimd.tensor_scalar_mul(out=s_ffn_sq_cube[:], in0=s_ffn_sq[:], scalar1=1.0 / CHANNELS**3)
            nc.gpsimd.tensor_scalar_mul(out=eps[:], in0=ones[:, 0:1], scalar1=EPS)
            nc.gpsimd.tensor_scalar_mul(out=shift[:], in0=shift_raw[:], scalar1=s_norm)
            nc.gpsimd.tensor_scalar(
                out=gain[:], in0=gain_raw[:], scalar1=s_norm, scalar2=s_ffn, op0=ALU.mult, op1=ALU.mult
            )

        def squares_on_scalar(i):
            return i % 4 != 3

        grouped = {}
        codes = {}
        scales = {}
        acc = {}
        v = {}
        stats = {}
        sums = {}
        mean = {}
        variance = {}
        neg_mean = {}
        inv_std = {}
        normed = {}
        turned = {}

        ordered = {}

        def order_words(i):
            ordered[i] = []
            for half in range(2):
                words = front.tile([P, 2, 2, P], F32, tag="ordered", name="ordered", bufs=6)
                nc.vector.tensor_copy(
                    out=words[:], in_=h_raw[i][half].bitcast(F32).rearrange("r (g p u) -> r g u p", g=2, u=2)
                )
                ordered[i].append(words)

        def transpose_h(i):
            grouped[i] = front.tile([P, PASSES * P * 4], BF16, tag="grouped", name="h_grouped", align_bytes=64)
            copiers = (nc.scalar.copy, nc.scalar.copy)
            if i in ORDERED:
                columns = [[[words[:, g, u, :] for u in range(2)] for g in range(2)] for words in ordered[i]]
            else:
                columns = [every_second_word(part) for part in h_raw[i]]
            k_to_partitions(nc, psum, columns, ident, grouped[i], copiers)

        def quantise_h(i):
            codes[i] = front.tile([P, PASSES * P], U32, tag="codes", name="h_codes", align_bytes=64, bufs=4)
            scales[i] = front.tile([P, PASSES * P], U8, tag="scales", name="h_scales", align_bytes=64, bufs=4)
            for half in range(2):
                nc.vector.quantize_mx(
                    out=codes[i][:, half * 2 * P : (half + 1) * 2 * P].bitcast(FP8X4),
                    scales=scales[i][:, half * 2 * P : (half + 1) * 2 * P],
                    in_=grouped[i][:, half * 8 * P : (half + 1) * 8 * P],
                )

        def multiply(i):
            acc[i] = psum.tile([P, CHANNELS], F32, tag="acc", name="acc")
            for g in range(PASSES):
                nc.tensor.matmul_mx(
                    out=acc[i][:],
                    lhsT=codes[i][:, g * P : (g + 1) * P].bitcast(FP8X4),
                    lhsT_scale=scales[i][:, g * P : (g + 1) * P],
                    rhs=w_codes[:, g, :].bitcast(FP8X4),
                    rhs_scale=w_scales[:, g, :],
                    start=(g == 0),
                    stop=(g == PASSES - 1),
                )

        def add_bias(i):
            v[i] = back.tile([P, CHANNELS], F32, tag="v", name="v", bufs=4)
            bias_row = bias_all[:].rearrange("p t r -> p (t r)")
            if squares_on_scalar(i):
                sums[i] = back.tile([P, 1], F32, tag="sums", name="sums", bufs=4)
                nc.vector.scalar_tensor_tensor(
                    out=v[i][:],
                    in0=acc[i][:],
                    scalar=1.0,
                    in1=bias_row,
                    op0=ALU.mult,
                    op1=ALU.add,
                    accum_out=sums[i][:],
                )
            else:
                nc.vector.tensor_tensor(out=v[i][:], in0=acc[i][:], in1=bias_row, op=ALU.add)

        def sum_up(i):
            if not squares_on_scalar(i):
                stats[i] = back.tile([P, 6], F32, tag="stats", name="stats", bufs=4)
                nc.vector.bn_stats(out=stats[i][:], in_=v[i][:])

        def find_spread(i):
            neg_mean[i] = back.tile([P, 1], F32, tag="neg_mean", name="neg_mean", bufs=4)
            if squares_on_scalar(i):
                squares = back.tile([P, CHANNELS], F32, tag="squares")
                square_sum = back.tile([P, 1], F32, tag="square_sum", bufs=4)
                nc.scalar.activation(
                    out=squares[:],
                    in_=v[i][:],
                    func=ACT.Square,
                    bias=sums[i][:],
                    scale=-float(CHANNELS),
                    accum_out=square_sum[:],
                )
                variance[i] = (square_sum[:], s_ffn_sq_cube[:])
                nc.gpsimd.tensor_scalar(
                    out=neg_mean[i][:], in0=sums[i][:], scalar1=-1.0 / CHANNELS, scalar2=0.0, op0=ALU.mult, op1=ALU.add
                )
            else:
                moments = back.tile([P, 2], F32, tag="moments", bufs=4)
                nc.vector.bn_aggr(out=moments[:], in_=stats[i][:])
                variance[i] = (moments[:, 1:2], s_ffn_sq[:])
                if i == TILES - 1:
                    mean[i] = moments[:, 0:1]
                else:
                    nc.gpsimd.tensor_scalar(
                        out=neg_mean[i][:], in0=moments[:, 0:1], scalar1=-1.0, scalar2=0.0, op0=ALU.mult, op1=ALU.add
                    )

        def invert(i):
            inv_std[i] = back.tile([P, 1], F32, tag="inv_std", name="inv_std", bufs=4)
            spread, scale = variance[i]
            nc.scalar.activation(out=inv_std[i][:], in_=spread, func=ACT.Abs_reciprocal_sqrt, bias=eps[:], scale=scale)

        def normalise(i):
            normed[i] = back.tile([P, CHANNELS], F32, tag="normed", name="normed", bufs=6)
            if i == TILES - 1:
                nc.vector.tensor_scalar(
                    out=normed[i][:], in0=v[i][:], scalar1=mean[i], scalar2=inv_std[i][:], op0=ALU.subtract, op1=ALU.mult
                )
            else:
                nc.gpsimd.tensor_scalar(
                    out=normed[i][:], in0=v[i][:], scalar1=neg_mean[i][:], scalar2=inv_std[i][:], op0=ALU.add, op1=ALU.mult
                )

        def turn_back(b):
            turned[b] = [
                psum.tile([P, 2, IMAGE_PIXELS], F32, tag="bank", name="turned%d" % half, bufs=TURN_BANKS)
                for half in range(2)
            ]
            for part in range(TILES_IMAGE):
                for t in range(CH_BLOCKS):
                    nc.tensor.transpose(
                        turned[b][t // 2][:, t % 2, part * P : (part + 1) * P],
                        normed[b * TILES_IMAGE + part][:, t * P : (t + 1) * P],
                        ident[:],
                    )

        def finish(b, half):
            blocks = (2 * half, 2 * half + 1)
            summed = image.tile([P, 2, IMAGE_PIXELS], F32, tag="summed", bufs=6)
            result = image.tile([P, 2, IMAGE_PIXELS], F32, tag="result", bufs=6)
            for j, t in enumerate(blocks):
                nc.vector.scalar_tensor_tensor(
                    out=summed[:, j, :],
                    in0=turned[b][t // 2][:, t % 2, :],
                    scalar=gain[:, t : t + 1],
                    in1=x_raw[b][:, t * IMAGE_PIXELS : (t + 1) * IMAGE_PIXELS],
                    op0=ALU.mult,
                    op1=ALU.add,
                )
            for j, t in enumerate(blocks):
                nc.scalar.activation(
                    out=result[:, j, :], in_=summed[:, j, :], func=ACT.Relu, bias=shift[:, t : t + 1], scale=1.0
                )
                nc.sync.dma_start(
                    out=out_images[:, b, t * IMAGE_PIXELS : (t + 1) * IMAGE_PIXELS], in_=result[:, j, :]
                )

        transpose_h(0)
        quantise_h(0)
        spread_constants()
        order_words(2)
        transpose_h(1)
        quantise_h(1)
        turned_in = {min(2 * b + 5, b + 6): b for b in range(IMAGES)}
        for i in range(TILES + 3):
            if i < TILES:
                multiply(i)
            if 0 <= i - 2 < TILES:
                normalise(i - 2)
            if i + 3 in ORDERED:
                order_words(i + 3)
            if i + AHEAD < TILES:
                transpose_h(i + AHEAD)
            if 0 <= i - 1 < TILES:
                invert(i - 1)
            if i in turned_in:
                turn_back(turned_in[i])
            if i - 1 in turned_in:
                finish(turned_in[i - 1], 1)
            if i < TILES:
                add_bias(i)
            if i in turned_in:
                finish(turned_in[i], 0)
            if i < TILES:
                sum_up(i)
            if i + AHEAD < TILES:
                quantise_h(i + AHEAD)
            if i < TILES:
                find_spread(i)


def load_rows(nc, pool, rows, name, pieces):
    width = K // pieces
    halves = []
    for piece in range(pieces):
        part = pool.tile([P, width], BF16, name="%s_%d" % (name, piece))
        nc.sync.dma_start(out=part[:], in_=rows[:, piece * width : (piece + 1) * width])
        for j in range(2 // pieces):
            halves.append(part[:, j * (K // 2) : (j + 1) * (K // 2)])
    return halves


def load_x(nc, pool, x_images, x_raw):
    b = len(x_raw)
    x_tile = pool.tile([P, CH_BLOCKS * IMAGE_PIXELS], BF16, name="x_raw%d" % b)
    nc.sync.dma_start(out=x_tile[:], in_=x_images[:, b, :])
    x_raw.append(x_tile)


def every_second_word(rows):
    words = rows.bitcast(F32)
    return [[words[:, g * WORDS_PASS + u : (g + 1) * WORDS_PASS : 2] for u in range(2)] for g in range(2)]


def k_to_partitions(nc, psum, columns, ident, grouped, copiers):
    grouped_words = grouped[:].bitcast(F32).rearrange("p (g r u) -> p g r u", g=PASSES, u=2)
    for half in range(2):
        bank = psum.tile([P, 2, 2, P], F32, tag="bank", bufs=TURN_BANKS)
        for g in range(2):
            for u in range(2):
                nc.tensor.transpose(bank[:, g, u, :], columns[half][g][u], ident[:])
        copiers[half](
            out=grouped_words[:, 2 * half : 2 * half + 2, :, :], in_=bank[:].rearrange("p g u r -> p g r u")
        )
